import numpy as np
import ml_dtypes


def mxq(x, axis, fmt="e4m3"):
    dtype, down = {"e4m3": (ml_dtypes.float8_e4m3fn, 7), "e5m2": (ml_dtypes.float8_e5m2, 14)}[fmt]
    v = np.moveaxis(np.asarray(x, np.float32).astype(ml_dtypes.bfloat16).astype(np.float64), axis, -1)
    blocks = v.reshape(v.shape[:-1] + (-1, 32))
    amax = np.abs(blocks).max(-1, keepdims=True)
    byte = np.maximum(np.where(amax > 0, np.frexp(amax)[1] - 1 + 127, 0) - down, 1)
    scale = np.exp2(byte - 127.0)
    codes = (blocks / scale).astype(np.float32).astype(dtype).astype(np.float64)
    return np.moveaxis((codes * scale).reshape(v.shape), -1, axis)


WIDE = False


def mx_kscale(k):
    if not WIDE:
        return np.ones(k)
    levels = np.array([10, -10, 5, -5, 0])
    a = np.random.permutation(np.resize(levels, k // 512 * 4)).reshape(k // 512, 4)
    idx = np.arange(k)
    return np.exp2(a[idx // 512, idx % 128 // 32])


BF16 = ml_dtypes.bfloat16


def bf(x):
    return np.asarray(x, np.float32).astype(BF16)


def f64(x):
    return np.asarray(x).astype(np.float64)


B, L, D, E, S, H = 2, 128, 128, 16, 32, 512
K = E * S


def softmax(v):
    e = np.exp(v - v.max(-1, keepdims=True))
    return e / e.sum(-1, keepdims=True)


def setup_inputs():
    s = mx_kscale(H)
    return {"h": bf(np.random.standard_normal((B, E, S, H)) * 0.6 * s),
            "w2": bf(np.random.standard_normal((E, H, D)) * 1.5 / np.sqrt(H) / s[:, None]),
            "b2": bf(np.random.standard_normal((E, D)) * 0.5),
            "logits": bf(np.random.standard_normal((B, L, E, S)) * 2.0)}


def reference(h, w2, b2, logits):
    eo = (mxq(f64(h), 3, "e4m3") @ mxq(f64(w2), 1, "e4m3")) + f64(b2)[:, None, :]
    eo = eo.reshape(B, K, D)
    c_w = softmax(f64(logits).reshape(B, L, K))
    return mxq(c_w, 2, "e4m3") @ mxq(eo, 1, "e4m3")

@@ -1,0 +1,170 @@
+import concourse.mybir as mybir
+from concourse.masks import make_identity
+
+F32 = mybir.dt.float32
+BF16 = mybir.dt.bfloat16
+U32 = mybir.dt.uint32
+I32 = mybir.dt.int32
+U8 = mybir.dt.uint8
+FP8X4 = mybir.dt.float8_e4m3fn_x4
+ACT = mybir.ActivationFunctionType
+ALU = mybir.AluOpType
+
+P = 128
+PACK = 4
+B, L, D, E, S, H = 2, 128, 128, 16, 32, 512
+K = E * S
+GROUPS = 4
+EG = E // GROUPS
+ZEROS = P - S
+
+FLOPS = 2 * B * E * S * H * D + 2 * B * L * K * D
+
+
+def tile_softmoe_pb_s_kernel(tc, h, w2, b2, logits, out):
+    nc = tc.nc
+    with tc.tile_pool(name="keep", bufs=1) as keep, tc.psum_pool(name="psum", bufs=1) as psum:
+        ident_f32 = keep.tile([P, P], F32)
+        make_identity(nc, ident_f32[:])
+        ident_bf = keep.tile([P, P], BF16)
+        make_identity(nc, ident_bf[:])
+
+        warm_in = keep.tile([P, 1], F32)
+        warm_out = keep.tile([P, 1], F32)
+        nc.vector.memset(warm_in[:], 0.0)
+        nc.scalar.activation(out=warm_out[:], in_=warm_in[:], func=ACT.Exp)
+
+        h_masked = [keep.tile([P, ZEROS + E * P], U32, align_bytes=64, name="h_masked%d" % b) for b in range(B)]
+        for b in range(B):
+            nc.vector.memset(h_masked[b][:].bitcast(I32), 0)
+
+        lg = keep.tile([P, B, K], BF16)
+        nc.sync.dma_start(out=lg[:], in_=logits.rearrange("b l e s -> l b (e s)"))
+        h_raw = [keep.tile([P, GROUPS * H], BF16, name="h_raw%d" % b) for b in range(B)]
+        for b in range(B):
+            nc.sync.dma_start(
+                out=h_raw[b][:].rearrange("p (g k) -> p g k", g=GROUPS),
+                in_=h[b].rearrange("(g i) s k -> (i s) g k", i=EG),
+            )
+        w2_raw = [keep.tile([P, EG, PACK, D], BF16, name="w2_raw%d" % g) for g in range(GROUPS)]
+        for g in range(GROUPS):
+            nc.sync.dma_start(
+                out=w2_raw[g][:].rearrange("p i j d -> p i (j d)"),
+                in_=w2[EG * g : EG * (g + 1)].rearrange("i (p j) d -> p i (j d)", j=PACK),
+            )
+        bias = keep.tile([P, GROUPS, D], BF16)
+        b2_by_i = b2.rearrange("(g i) d -> i g d", i=EG)
+        for i in range(EG):
+            nc.gpsimd.dma_start(
+                out=bias[S * i : S * (i + 1), :, :],
+                in_=b2_by_i[i : i + 1].to_broadcast([S, GROUPS, D]),
+            )
+
+        neg_max = keep.tile([P, B], F32)
+        nc.vector.tensor_reduce(out=neg_max[:], in_=lg[:], axis=mybir.AxisListType.X, op=ALU.max, negate=True)
+        ex = keep.tile([P, B, K], F32)
+        ex_sum = keep.tile([P, B], F32)
+        for b in range(B):
+            nc.scalar.activation(
+                out=ex[:, b, :],
+                in_=lg[:, b, :],
+                func=ACT.Exp,
+                bias=neg_max[:, b : b + 1],
+                scale=1.0,
+                accum_out=ex_sum[:, b : b + 1],
+            )
+        inv_sum = keep.tile([P, B], F32)
+        nc.vector.reciprocal(out=inv_sum[:], in_=ex_sum[:])
+        cw = keep.tile([P, B, K], BF16)
+        for b in range(B):
+            nc.vector.tensor_scalar(
+                out=cw[:, b, :], in0=ex[:, b, :], scalar1=inv_sum[:, b : b + 1], scalar2=None, op0=ALU.mult
+            )
+
+        h_words = [keep.tile([P, K], U32, align_bytes=64, name="h_words%d" % b) for b in range(B)]
+        h_scales = [keep.tile([P, K], U8, align_bytes=64, name="h_scales%d" % b) for b in range(B)]
+        for b in range(B):
+            h_pairs = h_raw[b][:].bitcast(F32).rearrange("p (g q u) -> p g u q", g=GROUPS, u=2)
+            h_grp = keep.tile([P, K * PACK], BF16, align_bytes=64, name="h_grp%d" % b)
+            h_grp_pairs = h_grp[:].bitcast(F32).rearrange("p (g r u) -> p g r u", g=GROUPS, u=2)
+            for half in range(2):
+                h_t = psum.tile([P, 2, 2, P], F32, name="h_t%d%d" % (b, half))
+                for g2 in range(2):
+                    for u in range(2):
+                        nc.tensor.transpose(h_t[:, g2, u, :], h_pairs[:, 2 * half + g2, u, :], ident_f32[:])
+                nc.scalar.copy(
+                    out=h_grp_pairs[:, 2 * half : 2 * half + 2],
+                    in_=h_t[:].rearrange("p g u r -> p g r u"),
+                )
+            nc.vector.quantize_mx(out=h_words[b][:].bitcast(FP8X4), scales=h_scales[b][:], in_=h_grp[:])
+            nc.vector.tensor_copy(
+                out=h_masked[b][:, ZEROS:].bitcast(I32).rearrange("p (j x) -> p j x", x=P)[:, :, 0:S],
+                in_=h_words[b][:].bitcast(I32).rearrange("p (j s) -> p j s", s=S),
+            )
+
+        cw_t = psum.tile([P, B, PACK, L], BF16)
+        for b in range(B):
+            for t in range(PACK):
+                nc.tensor.transpose(cw_t[:, b, t, :], cw[:, b, P * t : P * (t + 1)], ident_bf[:])
+        cw_grp = keep.tile([P, B, L, PACK], BF16, align_bytes=64)
+        nc.scalar.copy(out=cw_grp[:], in_=cw_t[:].rearrange("p b t l -> p b l t"))
+        cw_words = keep.tile([P, B * L], U32, align_bytes=64)
+        cw_scales = keep.tile([P, B * L], U8, align_bytes=64)
+        nc.vector.quantize_mx(
+            out=cw_words[:].bitcast(FP8X4), scales=cw_scales[:], in_=cw_grp[:].rearrange("p b l t -> p (b l t)")
+        )
+
+        eo_ps = [psum.tile([P, GROUPS, D], F32, name="eo_ps%d" % b) for b in range(B)]
+        for g in range(GROUPS):
+            w2_grp = keep.tile([P, EG, D, PACK], BF16, align_bytes=64, name="w2_grp%d" % g)
+            for i in range(EG):
+                dst = w2_grp[:, i].rearrange("p (c n) j -> p c j n", n=4)
+                src = w2_raw[g][:, i].rearrange("p j (c n) -> p c j n", n=4)
+                if i < EG // 2:
+                    nc.vector.tensor_copy(out=dst, in_=src)
+                else:
+                    nc.scalar.copy(out=dst, in_=src)
+            w2_words = keep.tile([P, EG * D], U32, align_bytes=64, name="w2_words%d" % g)
+            w2_scales = keep.tile([P, EG * D], U8, align_bytes=64, name="w2_scales%d" % g)
+            nc.vector.quantize_mx(
+                out=w2_words[:].bitcast(FP8X4), scales=w2_scales[:], in_=w2_grp[:].rearrange("p i d j -> p (i d j)")
+            )
+            for b in range(B):
+                for i in range(EG):
+                    first = ZEROS + P * (EG * g + i) - S * i
+                    nc.tensor.matmul_mx(
+                        out=eo_ps[b][:, g, :],
+                        lhsT=h_masked[b][:, first : first + P].bitcast(FP8X4),
+                        lhsT_scale=h_scales[b][:, P * g : P * (g + 1)],
+                        rhs=w2_words[:, D * i : D * (i + 1)].bitcast(FP8X4),
+                        rhs_scale=w2_scales[:, D * i : D * (i + 1)],
+                        start=(i == 0),
+                        stop=(i == EG - 1),
+                    )
+
+        out_ps = psum.tile([P, B, D], F32)
+        for b in range(B):
+            eo_grp = keep.tile([P, D, GROUPS], BF16, align_bytes=64, name="eo_grp%d" % b)
+            nc.vector.tensor_tensor(
+                out=eo_grp[:],
+                in0=eo_ps[b][:].rearrange("p g d -> p d g"),
+                in1=bias[:].rearrange("p g d -> p d g"),
+                op=ALU.add,
+            )
+            eo_words = keep.tile([P, D], U32, align_bytes=64, name="eo_words%d" % b)
+            eo_scales = keep.tile([P, D], U8, align_bytes=64, name="eo_scales%d" % b)
+            nc.vector.quantize_mx(
+                out=eo_words[:].bitcast(FP8X4), scales=eo_scales[:], in_=eo_grp[:].rearrange("p d g -> p (d g)")
+            )
+            nc.tensor.matmul_mx(
+                out=out_ps[:, b, :],
+                lhsT=cw_words[:, L * b : L * (b + 1)].bitcast(FP8X4),
+                lhsT_scale=cw_scales[:, L * b : L * (b + 1)],
+                rhs=eo_words[:].bitcast(FP8X4),
+                rhs_scale=eo_scales[:],
+                start=True,
+                stop=True,
+            )
+        out_sb = keep.tile([P, B, D], F32)
+        nc.scalar.copy(out=out_sb[:], in_=out_ps[:])
+        nc.sync.dma_start(out=out.rearrange("b l d -> l b d"), in_=out_sb[:])

@@ -17,6 +17,8 @@ K = E * S
 GROUPS = 4
 EG = E // GROUPS
 ZEROS = P - S
+PAIRS = E // 2
+VECTOR_ONLY_PAIRS = 2
 
 FLOPS = 2 * B * E * S * H * D + 2 * B * L * K * D
 
@@ -25,46 +27,49 @@ def tile_softmoe_pb_s_kernel(tc, h, w2, b2, logits, out):
     nc = tc.nc
     with tc.tile_pool(name="keep", bufs=1) as keep, tc.psum_pool(name="psum", bufs=1) as psum:
         ident_f32 = keep.tile([P, P], F32)
-        make_identity(nc, ident_f32[:])
         ident_bf = keep.tile([P, P], BF16)
-        make_identity(nc, ident_bf[:])
-
-        warm_in = keep.tile([P, 1], F32)
-        warm_out = keep.tile([P, 1], F32)
-        nc.vector.memset(warm_in[:], 0.0)
-        nc.scalar.activation(out=warm_out[:], in_=warm_in[:], func=ACT.Exp)
-
-        h_masked = [keep.tile([P, ZEROS + E * P], U32, align_bytes=64, name="h_masked%d" % b) for b in range(B)]
-        for b in range(B):
-            nc.vector.memset(h_masked[b][:].bitcast(I32), 0)
-
         lg = keep.tile([P, B, K], BF16)
-        nc.sync.dma_start(out=lg[:], in_=logits.rearrange("b l e s -> l b (e s)"))
         h_raw = [keep.tile([P, GROUPS * H], BF16, name="h_raw%d" % b) for b in range(B)]
-        for b in range(B):
+        h_grp = [keep.tile([P, K * PACK], BF16, align_bytes=64, name="h_grp%d" % b) for b in range(B)]
+        h_words = [keep.tile([P, K], U32, align_bytes=64, name="h_words%d" % b) for b in range(B)]
+        h_scales = [keep.tile([P, K], U8, align_bytes=64, name="h_scales%d" % b) for b in range(B)]
+        h_masked = [keep.tile([P, ZEROS + E * P], U32, align_bytes=64, name="h_masked%d" % b) for b in range(B)]
+        w2_raw = [keep.tile([P, 2, PACK, D], BF16, name="w2_raw%d" % c) for c in range(PAIRS)]
+        w2_grp = [keep.tile([P, 2, D, PACK], BF16, align_bytes=64, name="w2_grp%d" % c) for c in range(PAIRS)]
+        w2_words = [keep.tile([P, 2 * D], U32, align_bytes=64, name="w2_words%d" % c) for c in range(PAIRS)]
+        w2_scales = [keep.tile([P, 2 * D], U8, align_bytes=64, name="w2_scales%d" % c) for c in range(PAIRS)]
+        bias = keep.tile([P, GROUPS, D], BF16)
+        neg_max = keep.tile([P, B], F32)
+        ex = keep.tile([P, B, K], F32)
+        ex_sum = keep.tile([P, B], F32)
+        inv_sum = keep.tile([P, B], F32)
+        cw = keep.tile([P, B, K], BF16)
+        cw_grp = keep.tile([P, B, L, PACK], BF16, align_bytes=64)
+        cw_words = keep.tile([P, B * L], U32, align_bytes=64)
+        cw_scales = keep.tile([P, B * L], U8, align_bytes=64)
+        eo_ps = [psum.tile([P, GROUPS, D], F32, name="eo_ps%d" % b) for b in range(B)]
+
+        def load_logits(b):
+            nc.sync.dma_start(out=lg[:, b, :], in_=logits[b].rearrange("l e s -> l (e s)"))
+
+        def load_h(b):
             nc.sync.dma_start(
                 out=h_raw[b][:].rearrange("p (g k) -> p g k", g=GROUPS),
                 in_=h[b].rearrange("(g i) s k -> (i s) g k", i=EG),
             )
-        w2_raw = [keep.tile([P, EG, PACK, D], BF16, name="w2_raw%d" % g) for g in range(GROUPS)]
-        for g in range(GROUPS):
+
+        def load_pair(c):
             nc.sync.dma_start(
-                out=w2_raw[g][:].rearrange("p i j d -> p i (j d)"),
-                in_=w2[EG * g : EG * (g + 1)].rearrange("i (p j) d -> p i (j d)", j=PACK),
-            )
-        bias = keep.tile([P, GROUPS, D], BF16)
-        b2_by_i = b2.rearrange("(g i) d -> i g d", i=EG)
-        for i in range(EG):
-            nc.gpsimd.dma_start(
-                out=bias[S * i : S * (i + 1), :, :],
-                in_=b2_by_i[i : i + 1].to_broadcast([S, GROUPS, D]),
+                out=w2_raw[c][:].rearrange("p i j d -> p i (j d)"),
+                in_=w2[2 * c : 2 * c + 2].rearrange("i (p j) d -> p i (j d)", j=PACK),
             )
 
-        neg_max = keep.tile([P, B], F32)
-        nc.vector.tensor_reduce(out=neg_max[:], in_=lg[:], axis=mybir.AxisListType.X, op=ALU.max, negate=True)
-        ex = keep.tile([P, B, K], F32)
-        ex_sum = keep.tile([P, B], F32)
-        for b in range(B):
+        def softmax_max(b):
+            nc.vector.tensor_reduce(
+                out=neg_max[:, b : b + 1], in_=lg[:, b, :], axis=mybir.AxisListType.X, op=ALU.max, negate=True
+            )
+
+        def softmax_exp(b):
             nc.scalar.activation(
                 out=ex[:, b, :],
                 in_=lg[:, b, :],
@@ -73,22 +78,24 @@ def tile_softmoe_pb_s_kernel(tc, h, w2, b2, logits, out):
                 scale=1.0,
                 accum_out=ex_sum[:, b : b + 1],
             )
-        inv_sum = keep.tile([P, B], F32)
-        nc.vector.reciprocal(out=inv_sum[:], in_=ex_sum[:])
-        cw = keep.tile([P, B, K], BF16)
-        for b in range(B):
+
+        def softmax_normalise(b):
+            nc.vector.reciprocal(out=inv_sum[:, b : b + 1], in_=ex_sum[:, b : b + 1])
             nc.vector.tensor_scalar(
                 out=cw[:, b, :], in0=ex[:, b, :], scalar1=inv_sum[:, b : b + 1], scalar2=None, op0=ALU.mult
             )
 
-        h_words = [keep.tile([P, K], U32, align_bytes=64, name="h_words%d" % b) for b in range(B)]
-        h_scales = [keep.tile([P, K], U8, align_bytes=64, name="h_scales%d" % b) for b in range(B)]
-        for b in range(B):
+        def transpose_cw(b):
+            cw_t = psum.tile([P, PACK, L], BF16, name="cw_t%d" % b, tag="transposed", bufs=4)
+            for t in range(PACK):
+                nc.tensor.transpose(cw_t[:, t, :], cw[:, b, P * t : P * (t + 1)], ident_bf[:])
+            nc.scalar.copy(out=cw_grp[:, b], in_=cw_t[:].rearrange("p t l -> p l t"))
+
+        def transpose_h(b):
             h_pairs = h_raw[b][:].bitcast(F32).rearrange("p (g q u) -> p g u q", g=GROUPS, u=2)
-            h_grp = keep.tile([P, K * PACK], BF16, align_bytes=64, name="h_grp%d" % b)
-            h_grp_pairs = h_grp[:].bitcast(F32).rearrange("p (g r u) -> p g r u", g=GROUPS, u=2)
+            h_grp_pairs = h_grp[b][:].bitcast(F32).rearrange("p (g r u) -> p g r u", g=GROUPS, u=2)
             for half in range(2):
-                h_t = psum.tile([P, 2, 2, P], F32, name="h_t%d%d" % (b, half))
+                h_t = psum.tile([P, 2, 2, P], F32, name="h_t%d%d" % (b, half), tag="transposed", bufs=4)
                 for g2 in range(2):
                     for u in range(2):
                         nc.tensor.transpose(h_t[:, g2, u, :], h_pairs[:, 2 * half + g2, u, :], ident_f32[:])
@@ -96,75 +103,127 @@ def tile_softmoe_pb_s_kernel(tc, h, w2, b2, logits, out):
                     out=h_grp_pairs[:, 2 * half : 2 * half + 2],
                     in_=h_t[:].rearrange("p g u r -> p g r u"),
                 )
-            nc.vector.quantize_mx(out=h_words[b][:].bitcast(FP8X4), scales=h_scales[b][:], in_=h_grp[:])
+
+        def quantise_h(b):
+            nc.vector.quantize_mx(out=h_words[b][:].bitcast(FP8X4), scales=h_scales[b][:], in_=h_grp[b][:])
             nc.vector.tensor_copy(
                 out=h_masked[b][:, ZEROS:].bitcast(I32).rearrange("p (j x) -> p j x", x=P)[:, :, 0:S],
                 in_=h_words[b][:].bitcast(I32).rearrange("p (j s) -> p j s", s=S),
             )
 
-        cw_t = psum.tile([P, B, PACK, L], BF16)
-        for b in range(B):
-            for t in range(PACK):
-                nc.tensor.transpose(cw_t[:, b, t, :], cw[:, b, P * t : P * (t + 1)], ident_bf[:])
-        cw_grp = keep.tile([P, B, L, PACK], BF16, align_bytes=64)
-        nc.scalar.copy(out=cw_grp[:], in_=cw_t[:].rearrange("p b t l -> p b l t"))
-        cw_words = keep.tile([P, B * L], U32, align_bytes=64)
-        cw_scales = keep.tile([P, B * L], U8, align_bytes=64)
-        nc.vector.quantize_mx(
-            out=cw_words[:].bitcast(FP8X4), scales=cw_scales[:], in_=cw_grp[:].rearrange("p b l t -> p (b l t)")
-        )
-
-        eo_ps = [psum.tile([P, GROUPS, D], F32, name="eo_ps%d" % b) for b in range(B)]
-        for g in range(GROUPS):
-            w2_grp = keep.tile([P, EG, D, PACK], BF16, align_bytes=64, name="w2_grp%d" % g)
-            for i in range(EG):
-                dst = w2_grp[:, i].rearrange("p (c n) j -> p c j n", n=4)
-                src = w2_raw[g][:, i].rearrange("p j (c n) -> p c j n", n=4)
-                if i < EG // 2:
-                    nc.vector.tensor_copy(out=dst, in_=src)
-                else:
-                    nc.scalar.copy(out=dst, in_=src)
-            w2_words = keep.tile([P, EG * D], U32, align_bytes=64, name="w2_words%d" % g)
-            w2_scales = keep.tile([P, EG * D], U8, align_bytes=64, name="w2_scales%d" % g)
-            nc.vector.quantize_mx(
-                out=w2_words[:].bitcast(FP8X4), scales=w2_scales[:], in_=w2_grp[:].rearrange("p i d j -> p (i d j)")
+        def regroup_expert(engine_copy, c, i):
+            engine_copy(
+                out=w2_grp[c][:, i].rearrange("p (c n) j -> p c j n", n=4),
+                in_=w2_raw[c][:, i].rearrange("p j (c n) -> p c j n", n=4),
             )
+
+        def regroup_pair(c):
+            regroup_expert(nc.vector.tensor_copy, c, 0)
+            if c < VECTOR_ONLY_PAIRS:
+                regroup_expert(nc.vector.tensor_copy, c, 1)
+            else:
+                regroup_expert(nc.scalar.copy, c, 1)
+
+        def quantise_pair(c):
+            nc.vector.quantize_mx(
+                out=w2_words[c][:].bitcast(FP8X4),
+                scales=w2_scales[c][:],
+                in_=w2_grp[c][:].rearrange("p i d j -> p (i d j)"),
+            )
+
+        def expert_passes(c):
             for b in range(B):
-                for i in range(EG):
-                    first = ZEROS + P * (EG * g + i) - S * i
+                for e in (2 * c, 2 * c + 1):
+                    g, i = divmod(e, EG)
+                    first = ZEROS + P * e - S * i
                     nc.tensor.matmul_mx(
                         out=eo_ps[b][:, g, :],
                         lhsT=h_masked[b][:, first : first + P].bitcast(FP8X4),
                         lhsT_scale=h_scales[b][:, P * g : P * (g + 1)],
-                        rhs=w2_words[:, D * i : D * (i + 1)].bitcast(FP8X4),
-                        rhs_scale=w2_scales[:, D * i : D * (i + 1)],
+                        rhs=w2_words[c][:, D * (e - 2 * c) : D * (e - 2 * c + 1)].bitcast(FP8X4),
+                        rhs_scale=w2_scales[c][:, D * (e - 2 * c) : D * (e - 2 * c + 1)],
                         start=(i == 0),
                         stop=(i == EG - 1),
                     )
 
-        out_ps = psum.tile([P, B, D], F32)
+        load_logits(0)
+        load_logits(1)
+        load_pair(0)
+        load_h(0)
+        load_pair(1)
+        load_h(1)
+        for c in range(VECTOR_ONLY_PAIRS, PAIRS):
+            load_pair(c)
+        b2_by_i = b2.rearrange("(g i) d -> i g d", i=EG)
+        for i in range(EG):
+            nc.sync.dma_start(
+                out=bias[S * i : S * (i + 1), :, :],
+                in_=b2_by_i[i : i + 1].to_broadcast([S, GROUPS, D]),
+            )
+
+        make_identity(nc, ident_bf[:])
+        make_identity(nc, ident_f32[:])
+        warm_in = keep.tile([P, 1], F32)
+        warm_out = keep.tile([P, 1], F32)
+        nc.vector.memset(warm_in[:], 0.0)
+        nc.scalar.activation(out=warm_out[:], in_=warm_in[:], func=ACT.Exp)
         for b in range(B):
-            eo_grp = keep.tile([P, D, GROUPS], BF16, align_bytes=64, name="eo_grp%d" % b)
+            nc.vector.memset(h_masked[b][:].bitcast(I32), 0)
+
+        softmax_max(0)
+        softmax_max(1)
+        softmax_exp(0)
+        softmax_exp(1)
+        softmax_normalise(0)
+        regroup_pair(0)
+        softmax_normalise(1)
+        transpose_cw(0)
+        transpose_cw(1)
+        quantise_pair(0)
+        regroup_pair(1)
+        transpose_h(0)
+        nc.vector.quantize_mx(
+            out=cw_words[:].bitcast(FP8X4), scales=cw_scales[:], in_=cw_grp[:].rearrange("p b l t -> p (b l t)")
+        )
+        quantise_pair(1)
+        transpose_h(1)
+        quantise_h(0)
+        regroup_pair(2)
+        regroup_pair(3)
+        quantise_h(1)
+        expert_passes(0)
+        expert_passes(1)
+
+        for c in range(2, PAIRS):
+            if c + 2 < PAIRS:
+                regroup_pair(c + 2)
+            quantise_pair(c)
+            expert_passes(c)
+
+        eo_grp = [keep.tile([P, D, GROUPS], BF16, align_bytes=64, name="eo_grp%d" % b) for b in range(B)]
+        eo_words = [keep.tile([P, D], U32, align_bytes=64, name="eo_words%d" % b) for b in range(B)]
+        eo_scales = [keep.tile([P, D], U8, align_bytes=64, name="eo_scales%d" % b) for b in range(B)]
+        for b in range(B):
             nc.vector.tensor_tensor(
-                out=eo_grp[:],
+                out=eo_grp[b][:],
                 in0=eo_ps[b][:].rearrange("p g d -> p d g"),
                 in1=bias[:].rearrange("p g d -> p d g"),
                 op=ALU.add,
             )
-            eo_words = keep.tile([P, D], U32, align_bytes=64, name="eo_words%d" % b)
-            eo_scales = keep.tile([P, D], U8, align_bytes=64, name="eo_scales%d" % b)
+        for b in range(B):
             nc.vector.quantize_mx(
-                out=eo_words[:].bitcast(FP8X4), scales=eo_scales[:], in_=eo_grp[:].rearrange("p d g -> p (d g)")
+                out=eo_words[b][:].bitcast(FP8X4), scales=eo_scales[b][:], in_=eo_grp[b][:].rearrange("p d g -> p (d g)")
             )
+            out_ps = psum.tile([P, D], F32, name="out_ps%d" % b)
             nc.tensor.matmul_mx(
-                out=out_ps[:, b, :],
+                out=out_ps[:],
                 lhsT=cw_words[:, L * b : L * (b + 1)].bitcast(FP8X4),
                 lhsT_scale=cw_scales[:, L * b : L * (b + 1)],
-                rhs=eo_words[:].bitcast(FP8X4),
-                rhs_scale=eo_scales[:],
+                rhs=eo_words[b][:].bitcast(FP8X4),
+                rhs_scale=eo_scales[b][:],
                 start=True,
                 stop=True,
             )
-        out_sb = keep.tile([P, B, D], F32)
-        nc.scalar.copy(out=out_sb[:], in_=out_ps[:])
-        nc.sync.dma_start(out=out.rearrange("b l d -> l b d"), in_=out_sb[:])
+            out_sb = keep.tile([P, D], F32, name="out_sb%d" % b)
+            nc.scalar.copy(out=out_sb[:], in_=out_ps[:])
+            nc.sync.dma_start(out=out[b], in_=out_sb[:])

@@ -25,7 +25,7 @@ FLOPS = 2 * B * E * S * H * D + 2 * B * L * K * D
 
 def tile_softmoe_pb_s_kernel(tc, h, w2, b2, logits, out):
     nc = tc.nc
-    with tc.tile_pool(name="keep", bufs=1) as keep, tc.psum_pool(name="psum", bufs=1) as psum:
+    with tc.tile_pool(name="keep", bufs=1) as keep, tc.psum_pool(name="psum", bufs=1) as psum, tc.manual_schedule():
         ident_f32 = keep.tile([P, P], F32)
         ident_bf = keep.tile([P, P], BF16)
         lg = keep.tile([P, B, K], BF16)
@@ -33,7 +33,7 @@ def tile_softmoe_pb_s_kernel(tc, h, w2, b2, logits, out):
         h_grp = [keep.tile([P, K * PACK], BF16, align_bytes=64, name="h_grp%d" % b) for b in range(B)]
         h_words = [keep.tile([P, K], U32, align_bytes=64, name="h_words%d" % b) for b in range(B)]
         h_scales = [keep.tile([P, K], U8, align_bytes=64, name="h_scales%d" % b) for b in range(B)]
-        h_masked = [keep.tile([P, ZEROS + E * P], U32, align_bytes=64, name="h_masked%d" % b) for b in range(B)]
+        h_masked = [keep.tile([P, E * P], U32, align_bytes=64, name="h_masked%d" % b) for b in range(B)]
         w2_raw = [keep.tile([P, 2, PACK, D], BF16, name="w2_raw%d" % c) for c in range(PAIRS)]
         w2_grp = [keep.tile([P, 2, D, PACK], BF16, align_bytes=64, name="w2_grp%d" % c) for c in range(PAIRS)]
         w2_words = [keep.tile([P, 2 * D], U32, align_bytes=64, name="w2_words%d" % c) for c in range(PAIRS)]
@@ -47,15 +47,19 @@ def tile_softmoe_pb_s_kernel(tc, h, w2, b2, logits, out):
         cw_grp = keep.tile([P, B, L, PACK], BF16, align_bytes=64)
         cw_words = keep.tile([P, B * L], U32, align_bytes=64)
         cw_scales = keep.tile([P, B * L], U8, align_bytes=64)
+        eo_grp = [keep.tile([P, D, GROUPS], BF16, align_bytes=64, name="eo_grp%d" % b) for b in range(B)]
+        eo_words = [keep.tile([P, D], U32, align_bytes=64, name="eo_words%d" % b) for b in range(B)]
+        eo_scales = [keep.tile([P, D], U8, align_bytes=64, name="eo_scales%d" % b) for b in range(B)]
         eo_ps = [psum.tile([P, GROUPS, D], F32, name="eo_ps%d" % b) for b in range(B)]
 
         def load_logits(b):
             nc.sync.dma_start(out=lg[:, b, :], in_=logits[b].rearrange("l e s -> l (e s)"))
 
-        def load_h(b):
+        def load_h(b, half):
+            groups = slice(2 * half, 2 * half + 2)
             nc.sync.dma_start(
-                out=h_raw[b][:].rearrange("p (g k) -> p g k", g=GROUPS),
-                in_=h[b].rearrange("(g i) s k -> (i s) g k", i=EG),
+                out=h_raw[b][:].rearrange("p (g k) -> p g k", g=GROUPS)[:, groups, :],
+                in_=h[b].rearrange("(g i) s k -> (i s) g k", i=EG)[:, groups, :],
             )
 
         def load_pair(c):
@@ -91,6 +95,11 @@ def tile_softmoe_pb_s_kernel(tc, h, w2, b2, logits, out):
                 nc.tensor.transpose(cw_t[:, t, :], cw[:, b, P * t : P * (t + 1)], ident_bf[:])
             nc.scalar.copy(out=cw_grp[:, b], in_=cw_t[:].rearrange("p t l -> p l t"))
 
+        def quantise_cw():
+            nc.vector.quantize_mx(
+                out=cw_words[:].bitcast(FP8X4), scales=cw_scales[:], in_=cw_grp[:].rearrange("p b l t -> p (b l t)")
+            )
+
         def transpose_h(b):
             h_pairs = h_raw[b][:].bitcast(F32).rearrange("p (g q u) -> p g u q", g=GROUPS, u=2)
             h_grp_pairs = h_grp[b][:].bitcast(F32).rearrange("p (g r u) -> p g r u", g=GROUPS, u=2)
@@ -106,9 +115,11 @@ def tile_softmoe_pb_s_kernel(tc, h, w2, b2, logits, out):
 
         def quantise_h(b):
             nc.vector.quantize_mx(out=h_words[b][:].bitcast(FP8X4), scales=h_scales[b][:], in_=h_grp[b][:])
+
+        def mask_h(b):
             nc.vector.tensor_copy(
-                out=h_masked[b][:, ZEROS:].bitcast(I32).rearrange("p (j x) -> p j x", x=P)[:, :, 0:S],
-                in_=h_words[b][:].bitcast(I32).rearrange("p (j s) -> p j s", s=S),
+                out=h_masked[b][:].bitcast(I32).rearrange("p (e x) -> p e x", x=P)[:, :, ZEROS:P],
+                in_=h_words[b][:].bitcast(I32).rearrange("p (e s) -> p e s", s=S),
             )
 
         def regroup_expert(engine_copy, c, i):
@@ -131,28 +142,30 @@ def tile_softmoe_pb_s_kernel(tc, h, w2, b2, logits, out):
                 in_=w2_grp[c][:].rearrange("p i d j -> p (i d j)"),
             )
 
-        def expert_passes(c):
-            for b in range(B):
-                for e in (2 * c, 2 * c + 1):
-                    g, i = divmod(e, EG)
-                    first = ZEROS + P * e - S * i
-                    nc.tensor.matmul_mx(
-                        out=eo_ps[b][:, g, :],
-                        lhsT=h_masked[b][:, first : first + P].bitcast(FP8X4),
-                        lhsT_scale=h_scales[b][:, P * g : P * (g + 1)],
-                        rhs=w2_words[c][:, D * (e - 2 * c) : D * (e - 2 * c + 1)].bitcast(FP8X4),
-                        rhs_scale=w2_scales[c][:, D * (e - 2 * c) : D * (e - 2 * c + 1)],
-                        start=(i == 0),
-                        stop=(i == EG - 1),
-                    )
+        def expert_passes(c, b):
+            for n in range(2):
+                e = 2 * c + n
+                g, i = divmod(e, EG)
+                first = P * e + ZEROS - S * i
+                nc.tensor.matmul_mx(
+                    out=eo_ps[b][:, g, :],
+                    lhsT=h_masked[b][:, first : first + P].bitcast(FP8X4),
+                    lhsT_scale=h_scales[b][:, P * g : P * (g + 1)],
+                    rhs=w2_words[c][:, D * n : D * (n + 1)].bitcast(FP8X4),
+                    rhs_scale=w2_scales[c][:, D * n : D * (n + 1)],
+                    start=(i == 0),
+                    stop=(i == EG - 1),
+                )
 
         load_logits(0)
+        load_h(0, 0)
         load_logits(1)
+        load_h(0, 1)
         load_pair(0)
-        load_h(0)
+        load_h(1, 0)
         load_pair(1)
-        load_h(1)
-        for c in range(VECTOR_ONLY_PAIRS, PAIRS):
+        load_h(1, 1)
+        for c in range(2, PAIRS):
             load_pair(c)
         b2_by_i = b2.rearrange("(g i) d -> i g d", i=EG)
         for i in range(EG):
@@ -161,48 +174,46 @@ def tile_softmoe_pb_s_kernel(tc, h, w2, b2, logits, out):
                 in_=b2_by_i[i : i + 1].to_broadcast([S, GROUPS, D]),
             )
 
-        make_identity(nc, ident_bf[:])
         make_identity(nc, ident_f32[:])
+        make_identity(nc, ident_bf[:])
         warm_in = keep.tile([P, 1], F32)
         warm_out = keep.tile([P, 1], F32)
         nc.vector.memset(warm_in[:], 0.0)
         nc.scalar.activation(out=warm_out[:], in_=warm_in[:], func=ACT.Exp)
         for b in range(B):
-            nc.vector.memset(h_masked[b][:].bitcast(I32), 0)
+            nc.vector.memset(h_masked[b][:].bitcast(I32).rearrange("p (e x) -> p e x", x=P)[:, :, 0:ZEROS], 0)
 
         softmax_max(0)
         softmax_max(1)
         softmax_exp(0)
         softmax_exp(1)
         softmax_normalise(0)
-        regroup_pair(0)
         softmax_normalise(1)
-        transpose_cw(0)
-        transpose_cw(1)
-        quantise_pair(0)
-        regroup_pair(1)
-        transpose_h(0)
-        nc.vector.quantize_mx(
-            out=cw_words[:].bitcast(FP8X4), scales=cw_scales[:], in_=cw_grp[:].rearrange("p b l t -> p (b l t)")
-        )
-        quantise_pair(1)
-        transpose_h(1)
+        for b in range(B):
+            transpose_h(b)
+            transpose_cw(b)
+        regroup_pair(0)
         quantise_h(0)
+        quantise_pair(0)
+        mask_h(0)
+        regroup_pair(1)
         regroup_pair(2)
-        regroup_pair(3)
+        quantise_pair(1)
         quantise_h(1)
-        expert_passes(0)
-        expert_passes(1)
+        regroup_pair(3)
+        mask_h(1)
+        quantise_cw()
+        for b in range(B):
+            for c in range(2):
+                expert_passes(c, b)
 
         for c in range(2, PAIRS):
+            quantise_pair(c)
             if c + 2 < PAIRS:
                 regroup_pair(c + 2)
-            quantise_pair(c)
-            expert_passes(c)
+            for b in range(B):
+                expert_passes(c, b)
 
-        eo_grp = [keep.tile([P, D, GROUPS], BF16, align_bytes=64, name="eo_grp%d" % b) for b in range(B)]
-        eo_words = [keep.tile([P, D], U32, align_bytes=64, name="eo_words%d" % b) for b in range(B)]
-        eo_scales = [keep.tile([P, D], U8, align_bytes=64, name="eo_scales%d" % b) for b in range(B)]
         for b in range(B):
             nc.vector.tensor_tensor(
                 out=eo_grp[b][:],
@@ -214,6 +225,7 @@ def tile_softmoe_pb_s_kernel(tc, h, w2, b2, logits, out):
             nc.vector.quantize_mx(
                 out=eo_words[b][:].bitcast(FP8X4), scales=eo_scales[b][:], in_=eo_grp[b][:].rearrange("p d g -> p (d g)")
             )
+        for b in range(B):
             out_ps = psum.tile([P, D], F32, name="out_ps%d" % b)
             nc.tensor.matmul_mx(
                 out=out_ps[:],
@@ -225,5 +237,8 @@ def tile_softmoe_pb_s_kernel(tc, h, w2, b2, logits, out):
                 stop=True,
             )
             out_sb = keep.tile([P, D], F32, name="out_sb%d" % b)
-            nc.scalar.copy(out=out_sb[:], in_=out_ps[:])
+            if b == 0:
+                nc.scalar.copy(out=out_sb[:], in_=out_ps[:])
+            else:
+                nc.vector.tensor_copy(out=out_sb[:], in_=out_ps[:])
             nc.sync.dma_start(out=out[b], in_=out_sb[:])

@@ -18,7 +18,6 @@ GROUPS = 4
 EG = E // GROUPS
 ZEROS = P - S
 PAIRS = E // 2
-VECTOR_ONLY_PAIRS = 2
 
 FLOPS = 2 * B * E * S * H * D + 2 * B * L * K * D
 
@@ -93,25 +92,26 @@ def tile_softmoe_pb_s_kernel(tc, h, w2, b2, logits, out):
             cw_t = psum.tile([P, PACK, L], BF16, name="cw_t%d" % b, tag="transposed", bufs=4)
             for t in range(PACK):
                 nc.tensor.transpose(cw_t[:, t, :], cw[:, b, P * t : P * (t + 1)], ident_bf[:])
-            nc.scalar.copy(out=cw_grp[:, b], in_=cw_t[:].rearrange("p t l -> p l t"))
+            return cw_t
 
-        def quantise_cw():
+        def quantise_cw(cw_t):
+            for b in range(B):
+                nc.scalar.copy(out=cw_grp[:, b], in_=cw_t[b][:].rearrange("p t l -> p l t"))
             nc.vector.quantize_mx(
                 out=cw_words[:].bitcast(FP8X4), scales=cw_scales[:], in_=cw_grp[:].rearrange("p b l t -> p (b l t)")
             )
 
-        def transpose_h(b):
+        def transpose_h(b, half):
             h_pairs = h_raw[b][:].bitcast(F32).rearrange("p (g q u) -> p g u q", g=GROUPS, u=2)
             h_grp_pairs = h_grp[b][:].bitcast(F32).rearrange("p (g r u) -> p g r u", g=GROUPS, u=2)
-            for half in range(2):
-                h_t = psum.tile([P, 2, 2, P], F32, name="h_t%d%d" % (b, half), tag="transposed", bufs=4)
-                for g2 in range(2):
-                    for u in range(2):
-                        nc.tensor.transpose(h_t[:, g2, u, :], h_pairs[:, 2 * half + g2, u, :], ident_f32[:])
-                nc.scalar.copy(
-                    out=h_grp_pairs[:, 2 * half : 2 * half + 2],
-                    in_=h_t[:].rearrange("p g u r -> p g r u"),
-                )
+            h_t = psum.tile([P, 2, 2, P], F32, name="h_t%d%d" % (b, half), tag="transposed", bufs=4)
+            for g2 in range(2):
+                for u in range(2):
+                    nc.tensor.transpose(h_t[:, g2, u, :], h_pairs[:, 2 * half + g2, u, :], ident_f32[:])
+            nc.scalar.copy(
+                out=h_grp_pairs[:, 2 * half : 2 * half + 2],
+                in_=h_t[:].rearrange("p g u r -> p g r u"),
+            )
 
         def quantise_h(b):
             nc.vector.quantize_mx(out=h_words[b][:].bitcast(FP8X4), scales=h_scales[b][:], in_=h_grp[b][:])
@@ -130,10 +130,7 @@ def tile_softmoe_pb_s_kernel(tc, h, w2, b2, logits, out):
 
         def regroup_pair(c):
             regroup_expert(nc.vector.tensor_copy, c, 0)
-            if c < VECTOR_ONLY_PAIRS:
-                regroup_expert(nc.vector.tensor_copy, c, 1)
-            else:
-                regroup_expert(nc.scalar.copy, c, 1)
+            regroup_expert(nc.scalar.copy, c, 1)
 
         def quantise_pair(c):
             nc.vector.quantize_mx(
@@ -161,11 +158,10 @@ def tile_softmoe_pb_s_kernel(tc, h, w2, b2, logits, out):
         load_h(0, 0)
         load_logits(1)
         load_h(0, 1)
-        load_pair(0)
         load_h(1, 0)
-        load_pair(1)
+        load_pair(0)
         load_h(1, 1)
-        for c in range(2, PAIRS):
+        for c in range(1, PAIRS):
             load_pair(c)
         b2_by_i = b2.rearrange("(g i) d -> i g d", i=EG)
         for i in range(EG):
@@ -189,22 +185,23 @@ def tile_softmoe_pb_s_kernel(tc, h, w2, b2, logits, out):
         softmax_exp(1)
         softmax_normalise(0)
         softmax_normalise(1)
-        for b in range(B):
-            transpose_h(b)
-            transpose_cw(b)
+        transpose_h(0, 0)
+        transpose_h(0, 1)
+        transpose_h(1, 0)
         regroup_pair(0)
+        transpose_h(1, 1)
+        cw_t = [transpose_cw(b) for b in range(B)]
         quantise_h(0)
-        quantise_pair(0)
-        mask_h(0)
         regroup_pair(1)
+        mask_h(0)
+        quantise_pair(0)
         regroup_pair(2)
-        quantise_pair(1)
         quantise_h(1)
-        regroup_pair(3)
+        quantise_pair(1)
         mask_h(1)
-        quantise_cw()
-        for b in range(B):
-            for c in range(2):
+        regroup_pair(3)
+        for c in range(2):
+            for b in range(B):
                 expert_passes(c, b)
 
         for c in range(2, PAIRS):
@@ -213,6 +210,8 @@ def tile_softmoe_pb_s_kernel(tc, h, w2, b2, logits, out):
                 regroup_pair(c + 2)
             for b in range(B):
                 expert_passes(c, b)
+
+        quantise_cw(cw_t)
 
         for b in range(B):
             nc.vector.tensor_tensor(

@@ -17,6 +17,7 @@ K = E * S
 GROUPS = 4
 EG = E // GROUPS
 ZEROS = P - S
+ROWS = K // P
 PAIRS = E // 2
 
 FLOPS = 2 * B * E * S * H * D + 2 * B * L * K * D
@@ -28,6 +29,7 @@ def tile_softmoe_pb_s_kernel(tc, h, w2, b2, logits, out):
         ident_f32 = keep.tile([P, P], F32)
         ident_bf = keep.tile([P, P], BF16)
         lg = keep.tile([P, B, K], BF16)
+        lg_neg = keep.tile([P, B, K], BF16)
         h_raw = [keep.tile([P, GROUPS * H], BF16, name="h_raw%d" % b) for b in range(B)]
         h_grp = [keep.tile([P, K * PACK], BF16, align_bytes=64, name="h_grp%d" % b) for b in range(B)]
         h_words = [keep.tile([P, K], U32, align_bytes=64, name="h_words%d" % b) for b in range(B)]
@@ -55,10 +57,10 @@ def tile_softmoe_pb_s_kernel(tc, h, w2, b2, logits, out):
             nc.sync.dma_start(out=lg[:, b, :], in_=logits[b].rearrange("l e s -> l (e s)"))
 
         def load_h(b, half):
-            groups = slice(2 * half, 2 * half + 2)
+            rows = slice(2 * half, 2 * half + 2)
             nc.sync.dma_start(
-                out=h_raw[b][:].rearrange("p (g k) -> p g k", g=GROUPS)[:, groups, :],
-                in_=h[b].rearrange("(g i) s k -> (i s) g k", i=EG)[:, groups, :],
+                out=h_raw[b][:].rearrange("p (r k) -> p r k", r=ROWS)[:, rows, :],
+                in_=h[b].rearrange("e s k -> (e s) k").rearrange("(p r) k -> p r k", r=ROWS)[:, rows, :],
             )
 
         def load_pair(c):
@@ -68,8 +70,14 @@ def tile_softmoe_pb_s_kernel(tc, h, w2, b2, logits, out):
             )
 
         def softmax_max(b):
-            nc.vector.tensor_reduce(
-                out=neg_max[:, b : b + 1], in_=lg[:, b, :], axis=mybir.AxisListType.X, op=ALU.max, negate=True
+            nc.vector.tensor_scalar(
+                out=lg_neg[:, b, :],
+                in0=lg[:, b, :],
+                scalar1=-1.0,
+                scalar2=None,
+                op0=ALU.mult,
+                op1=ALU.min,
+                accum_out=neg_max[:, b : b + 1],
             )
 
         def softmax_exp(b):
@@ -102,15 +110,15 @@ def tile_softmoe_pb_s_kernel(tc, h, w2, b2, logits, out):
             )
 
         def transpose_h(b, half):
-            h_pairs = h_raw[b][:].bitcast(F32).rearrange("p (g q u) -> p g u q", g=GROUPS, u=2)
-            h_grp_pairs = h_grp[b][:].bitcast(F32).rearrange("p (g r u) -> p g r u", g=GROUPS, u=2)
+            h_pairs = h_raw[b][:].bitcast(F32).rearrange("p (r q u) -> p r u q", r=ROWS, u=2)
+            h_grp_pairs = h_grp[b][:].bitcast(F32).rearrange("p (m r u) -> p m r u", r=ROWS, u=2)
             h_t = psum.tile([P, 2, 2, P], F32, name="h_t%d%d" % (b, half), tag="transposed", bufs=4)
-            for g2 in range(2):
+            for r2 in range(2):
                 for u in range(2):
-                    nc.tensor.transpose(h_t[:, g2, u, :], h_pairs[:, 2 * half + g2, u, :], ident_f32[:])
+                    nc.tensor.transpose(h_t[:, r2, u, :], h_pairs[:, 2 * half + r2, u, :], ident_f32[:])
             nc.scalar.copy(
-                out=h_grp_pairs[:, 2 * half : 2 * half + 2],
-                in_=h_t[:].rearrange("p g u r -> p g r u"),
+                out=h_grp_pairs[:, :, 2 * half : 2 * half + 2, :],
+                in_=h_t[:].rearrange("p r u m -> p m r u"),
             )
 
         def quantise_h(b):

@@ -27,7 +27,6 @@ def tile_softmoe_pb_s_kernel(tc, h, w2, b2, logits, out):
     nc = tc.nc
     with tc.tile_pool(name="keep", bufs=1) as keep, tc.psum_pool(name="psum", bufs=1) as psum, tc.manual_schedule():
         ident_f32 = keep.tile([P, P], F32)
-        ident_bf = keep.tile([P, P], BF16)
         lg = keep.tile([P, B, K], BF16)
         lg_neg = keep.tile([P, B, K], BF16)
         h_raw = [keep.tile([P, GROUPS * H], BF16, name="h_raw%d" % b) for b in range(B)]
@@ -45,12 +44,13 @@ def tile_softmoe_pb_s_kernel(tc, h, w2, b2, logits, out):
         ex_sum = keep.tile([P, B], F32)
         inv_sum = keep.tile([P, B], F32)
         cw = keep.tile([P, B, K], BF16)
-        cw_grp = keep.tile([P, B, L, PACK], BF16, align_bytes=64)
+        cw_grp = keep.tile([P, B * L * PACK], BF16, align_bytes=64)
         cw_words = keep.tile([P, B * L], U32, align_bytes=64)
         cw_scales = keep.tile([P, B * L], U8, align_bytes=64)
         eo_grp = [keep.tile([P, D, GROUPS], BF16, align_bytes=64, name="eo_grp%d" % b) for b in range(B)]
         eo_words = [keep.tile([P, D], U32, align_bytes=64, name="eo_words%d" % b) for b in range(B)]
         eo_scales = [keep.tile([P, D], U8, align_bytes=64, name="eo_scales%d" % b) for b in range(B)]
+        cw_t = psum.tile([P, B, 2, L], F32)
         eo_ps = [psum.tile([P, GROUPS, D], F32, name="eo_ps%d" % b) for b in range(B)]
 
         def load_logits(b):
@@ -93,21 +93,24 @@ def tile_softmoe_pb_s_kernel(tc, h, w2, b2, logits, out):
         def softmax_normalise(b):
             nc.vector.reciprocal(out=inv_sum[:, b : b + 1], in_=ex_sum[:, b : b + 1])
             nc.vector.tensor_scalar(
-                out=cw[:, b, :], in0=ex[:, b, :], scalar1=inv_sum[:, b : b + 1], scalar2=None, op0=ALU.mult
+                out=cw[:, b, :].rearrange("p (v m u) -> p v m u", v=2, u=2),
+                in0=ex[:, b, :].rearrange("p (v u m) -> p v m u", v=2, u=2),
+                scalar1=inv_sum[:, b : b + 1],
+                scalar2=None,
+                op0=ALU.mult,
             )
 
         def transpose_cw(b):
-            cw_t = psum.tile([P, PACK, L], BF16, name="cw_t%d" % b, tag="transposed", bufs=4)
-            for t in range(PACK):
-                nc.tensor.transpose(cw_t[:, t, :], cw[:, b, P * t : P * (t + 1)], ident_bf[:])
-            return cw_t
+            cw_pairs = cw[:, b, :].bitcast(F32)
+            for v in range(2):
+                nc.tensor.transpose(cw_t[:, b, v, :], cw_pairs[:, P * v : P * (v + 1)], ident_f32[:])
 
-        def quantise_cw(cw_t):
-            for b in range(B):
-                nc.scalar.copy(out=cw_grp[:, b], in_=cw_t[b][:].rearrange("p t l -> p l t"))
-            nc.vector.quantize_mx(
-                out=cw_words[:].bitcast(FP8X4), scales=cw_scales[:], in_=cw_grp[:].rearrange("p b l t -> p (b l t)")
+        def quantise_cw():
+            nc.scalar.copy(
+                out=cw_grp[:].bitcast(F32).rearrange("p (b l v) -> p b l v", b=B, v=2),
+                in_=cw_t[:].rearrange("p b v l -> p b l v"),
             )
+            nc.vector.quantize_mx(out=cw_words[:].bitcast(FP8X4), scales=cw_scales[:], in_=cw_grp[:])
 
         def transpose_h(b, half):
             h_pairs = h_raw[b][:].bitcast(F32).rearrange("p (r q u) -> p r u q", r=ROWS, u=2)
@@ -179,7 +182,6 @@ def tile_softmoe_pb_s_kernel(tc, h, w2, b2, logits, out):
             )
 
         make_identity(nc, ident_f32[:])
-        make_identity(nc, ident_bf[:])
         warm_in = keep.tile([P, 1], F32)
         warm_out = keep.tile([P, 1], F32)
         nc.vector.memset(warm_in[:], 0.0)
@@ -198,7 +200,8 @@ def tile_softmoe_pb_s_kernel(tc, h, w2, b2, logits, out):
         transpose_h(1, 0)
         regroup_pair(0)
         transpose_h(1, 1)
-        cw_t = [transpose_cw(b) for b in range(B)]
+        for b in range(B):
+            transpose_cw(b)
         quantise_h(0)
         regroup_pair(1)
         mask_h(0)
@@ -219,7 +222,7 @@ def tile_softmoe_pb_s_kernel(tc, h, w2, b2, logits, out):
             for b in range(B):
                 expert_passes(c, b)
 
-        quantise_cw(cw_t)
+        quantise_cw()
 
         for b in range(B):
             nc.vector.tensor_tensor(
@@ -233,7 +236,7 @@ def tile_softmoe_pb_s_kernel(tc, h, w2, b2, logits, out):
                 out=eo_words[b][:].bitcast(FP8X4), scales=eo_scales[b][:], in_=eo_grp[b][:].rearrange("p d g -> p (d g)")
             )
         for b in range(B):
-            out_ps = psum.tile([P, D], F32, name="out_ps%d" % b)
+            out_ps = psum.tile([P, D], F32, name="out_ps%d" % b, tag="transposed", bufs=4)
             nc.tensor.matmul_mx(
                 out=out_ps[:],
                 lhsT=cw_words[:, L * b : L * (b + 1)].bitcast(FP8X4),

@@ -63,10 +63,10 @@ def tile_softmoe_pb_s_kernel(tc, h, w2, b2, logits, out):
                 in_=h[b].rearrange("e s k -> (e s) k").rearrange("(p r) k -> p r k", r=ROWS)[:, rows, :],
             )
 
-        def load_pair(c):
+        def load_w2(c, i0, i1):
             nc.sync.dma_start(
-                out=w2_raw[c][:].rearrange("p i j d -> p i (j d)"),
-                in_=w2[2 * c : 2 * c + 2].rearrange("i (p j) d -> p i (j d)", j=PACK),
+                out=w2_raw[c][:, i0:i1].rearrange("p i j d -> p i (j d)"),
+                in_=w2[2 * c + i0 : 2 * c + i1].rearrange("i (p j) d -> p i (j d)", j=PACK),
             )
 
         def softmax_max(b):
@@ -143,11 +143,11 @@ def tile_softmoe_pb_s_kernel(tc, h, w2, b2, logits, out):
             regroup_expert(nc.vector.tensor_copy, c, 0)
             regroup_expert(nc.scalar.copy, c, 1)
 
-        def quantise_pair(c):
+        def quantise_w2(c, i0, i1):
             nc.vector.quantize_mx(
-                out=w2_words[c][:].bitcast(FP8X4),
-                scales=w2_scales[c][:],
-                in_=w2_grp[c][:].rearrange("p i d j -> p (i d j)"),
+                out=w2_words[c][:, D * i0 : D * i1].bitcast(FP8X4),
+                scales=w2_scales[c][:, D * i0 : D * i1],
+                in_=w2_grp[c][:, i0:i1].rearrange("p i d j -> p (i d j)"),
             )
 
         def expert_passes(c, b):
@@ -170,10 +170,12 @@ def tile_softmoe_pb_s_kernel(tc, h, w2, b2, logits, out):
         load_logits(1)
         load_h(0, 1)
         load_h(1, 0)
-        load_pair(0)
+        load_w2(0, 0, 2)
         load_h(1, 1)
-        for c in range(1, PAIRS):
-            load_pair(c)
+        for c in range(1, PAIRS - 1):
+            load_w2(c, 0, 2)
+        for i in range(2):
+            load_w2(PAIRS - 1, i, i + 1)
         b2_by_i = b2.rearrange("(g i) d -> i g d", i=EG)
         for i in range(EG):
             nc.sync.dma_start(
@@ -205,21 +207,26 @@ def tile_softmoe_pb_s_kernel(tc, h, w2, b2, logits, out):
         quantise_h(0)
         regroup_pair(1)
         mask_h(0)
-        quantise_pair(0)
+        quantise_w2(0, 0, 2)
         regroup_pair(2)
         quantise_h(1)
-        quantise_pair(1)
+        quantise_w2(1, 0, 2)
         mask_h(1)
         regroup_pair(3)
         for c in range(2):
             for b in range(B):
                 expert_passes(c, b)
 
-        for c in range(2, PAIRS):
-            quantise_pair(c)
-            if c + 2 < PAIRS:
-                regroup_pair(c + 2)
+        for c in range(2, PAIRS - 2):
+            quantise_w2(c, 0, 2)
+            regroup_pair(c + 2)
             for b in range(B):
+                expert_passes(c, b)
+        quantise_w2(PAIRS - 2, 0, 2)
+        for i in range(2):
+            quantise_w2(PAIRS - 1, i, i + 1)
+        for b in range(B):
+            for c in (PAIRS - 2, PAIRS - 1):
                 expert_passes(c, b)
 
         quantise_cw()

import concourse.mybir as mybir
from concourse.masks import make_identity

F32 = mybir.dt.float32
BF16 = mybir.dt.bfloat16
U32 = mybir.dt.uint32
I32 = mybir.dt.int32
U8 = mybir.dt.uint8
FP8X4 = mybir.dt.float8_e4m3fn_x4
ACT = mybir.ActivationFunctionType
ALU = mybir.AluOpType

P = 128
PACK = 4
B, L, D, E, S, H = 2, 128, 128, 16, 32, 512
K = E * S
GROUPS = 4
EG = E // GROUPS
ZEROS = P - S
ROWS = K // P
PAIRS = E // 2

FLOPS = 2 * B * E * S * H * D + 2 * B * L * K * D


def tile_softmoe_pb_s_kernel(tc, h, w2, b2, logits, out):
    nc = tc.nc
    with tc.tile_pool(name="keep", bufs=1) as keep, tc.psum_pool(name="psum", bufs=1) as psum, tc.manual_schedule():
        ident_f32 = keep.tile([P, P], F32)
        lg = keep.tile([P, B, K], BF16)
        lg_neg = keep.tile([P, B, K], BF16)
        h_raw = [keep.tile([P, GROUPS * H], BF16, name="h_raw%d" % b) for b in range(B)]
        h_grp = [keep.tile([P, K * PACK], BF16, align_bytes=64, name="h_grp%d" % b) for b in range(B)]
        h_words = [keep.tile([P, K], U32, align_bytes=64, name="h_words%d" % b) for b in range(B)]
        h_scales = [keep.tile([P, K], U8, align_bytes=64, name="h_scales%d" % b) for b in range(B)]
        h_masked = [keep.tile([P, E * P], U32, align_bytes=64, name="h_masked%d" % b) for b in range(B)]
        w2_raw = [keep.tile([P, 2, PACK, D], BF16, name="w2_raw%d" % c) for c in range(PAIRS)]
        w2_grp = [keep.tile([P, 2, D, PACK], BF16, align_bytes=64, name="w2_grp%d" % c) for c in range(PAIRS)]
        w2_words = [keep.tile([P, 2 * D], U32, align_bytes=64, name="w2_words%d" % c) for c in range(PAIRS)]
        w2_scales = [keep.tile([P, 2 * D], U8, align_bytes=64, name="w2_scales%d" % c) for c in range(PAIRS)]
        bias = keep.tile([P, GROUPS, D], BF16)
        neg_max = keep.tile([P, B], F32)
        ex = keep.tile([P, B, K], F32)
        ex_sum = keep.tile([P, B], F32)
        inv_sum = keep.tile([P, B], F32)
        cw = keep.tile([P, B, K], BF16)
        cw_grp = keep.tile([P, B * L * PACK], BF16, align_bytes=64)
        cw_words = keep.tile([P, B * L], U32, align_bytes=64)
        cw_scales = keep.tile([P, B * L], U8, align_bytes=64)
        eo_grp = [keep.tile([P, D, GROUPS], BF16, align_bytes=64, name="eo_grp%d" % b) for b in range(B)]
        eo_words = [keep.tile([P, D], U32, align_bytes=64, name="eo_words%d" % b) for b in range(B)]
        eo_scales = [keep.tile([P, D], U8, align_bytes=64, name="eo_scales%d" % b) for b in range(B)]
        cw_t = psum.tile([P, B, 2, L], F32)
        eo_ps = [psum.tile([P, GROUPS, D], F32, name="eo_ps%d" % b) for b in range(B)]

        def load_logits(b):
            nc.sync.dma_start(out=lg[:, b, :], in_=logits[b].rearrange("l e s -> l (e s)"))

        def load_h(b, half):
            rows = slice(2 * half, 2 * half + 2)
            nc.sync.dma_start(
                out=h_raw[b][:].rearrange("p (r k) -> p r k", r=ROWS)[:, rows, :],
                in_=h[b].rearrange("e s k -> (e s) k").rearrange("(p r) k -> p r k", r=ROWS)[:, rows, :],
            )

        def load_w2(c, i0, i1):
            nc.sync.dma_start(
                out=w2_raw[c][:, i0:i1].rearrange("p i j d -> p i (j d)"),
                in_=w2[2 * c + i0 : 2 * c + i1].rearrange("i (p j) d -> p i (j d)", j=PACK),
            )

        def softmax_max(b):
            nc.vector.tensor_scalar(
                out=lg_neg[:, b, :],
                in0=lg[:, b, :],
                scalar1=-1.0,
                scalar2=None,
                op0=ALU.mult,
                op1=ALU.min,
                accum_out=neg_max[:, b : b + 1],
            )

        def softmax_exp(b):
            nc.scalar.activation(
                out=ex[:, b, :],
                in_=lg[:, b, :],
                func=ACT.Exp,
                bias=neg_max[:, b : b + 1],
                scale=1.0,
                accum_out=ex_sum[:, b : b + 1],
            )

        def softmax_normalise(b):
            nc.vector.reciprocal(out=inv_sum[:, b : b + 1], in_=ex_sum[:, b : b + 1])
            nc.vector.tensor_scalar(
                out=cw[:, b, :].rearrange("p (v m u) -> p v m u", v=2, u=2),
                in0=ex[:, b, :].rearrange("p (v u m) -> p v m u", v=2, u=2),
                scalar1=inv_sum[:, b : b + 1],
                scalar2=None,
                op0=ALU.mult,
            )

        def transpose_cw(b):
            cw_pairs = cw[:, b, :].bitcast(F32)
            for v in range(2):
                nc.tensor.transpose(cw_t[:, b, v, :], cw_pairs[:, P * v : P * (v + 1)], ident_f32[:])

        def quantise_cw():
            nc.scalar.copy(
                out=cw_grp[:].bitcast(F32).rearrange("p (b l v) -> p b l v", b=B, v=2),
                in_=cw_t[:].rearrange("p b v l -> p b l v"),
            )
            nc.vector.quantize_mx(out=cw_words[:].bitcast(FP8X4), scales=cw_scales[:], in_=cw_grp[:])

        def transpose_h(b, half):
            h_pairs = h_raw[b][:].bitcast(F32).rearrange("p (r q u) -> p r u q", r=ROWS, u=2)
            h_grp_pairs = h_grp[b][:].bitcast(F32).rearrange("p (m r u) -> p m r u", r=ROWS, u=2)
            h_t = psum.tile([P, 2, 2, P], F32, name="h_t%d%d" % (b, half), tag="transposed", bufs=4)
            for r2 in range(2):
                for u in range(2):
                    nc.tensor.transpose(h_t[:, r2, u, :], h_pairs[:, 2 * half + r2, u, :], ident_f32[:])
            nc.scalar.copy(
                out=h_grp_pairs[:, :, 2 * half : 2 * half + 2, :],
                in_=h_t[:].rearrange("p r u m -> p m r u"),
            )

        def quantise_h(b):
            nc.vector.quantize_mx(out=h_words[b][:].bitcast(FP8X4), scales=h_scales[b][:], in_=h_grp[b][:])

        def mask_h(b):
            nc.vector.tensor_copy(
                out=h_masked[b][:].bitcast(I32).rearrange("p (e x) -> p e x", x=P)[:, :, ZEROS:P],
                in_=h_words[b][:].bitcast(I32).rearrange("p (e s) -> p e s", s=S),
            )

        def regroup_expert(engine_copy, c, i):
            engine_copy(
                out=w2_grp[c][:, i].rearrange("p (c n) j -> p c j n", n=4),
                in_=w2_raw[c][:, i].rearrange("p j (c n) -> p c j n", n=4),
            )

        def regroup_pair(c):
            regroup_expert(nc.vector.tensor_copy, c, 0)
            regroup_expert(nc.scalar.copy, c, 1)

        def quantise_w2(c, i0, i1):
            nc.vector.quantize_mx(
                out=w2_words[c][:, D * i0 : D * i1].bitcast(FP8X4),
                scales=w2_scales[c][:, D * i0 : D * i1],
                in_=w2_grp[c][:, i0:i1].rearrange("p i d j -> p (i d j)"),
            )

        def expert_passes(c, b):
            for n in range(2):
                e = 2 * c + n
                g, i = divmod(e, EG)
                first = P * e + ZEROS - S * i
                nc.tensor.matmul_mx(
                    out=eo_ps[b][:, g, :],
                    lhsT=h_masked[b][:, first : first + P].bitcast(FP8X4),
                    lhsT_scale=h_scales[b][:, P * g : P * (g + 1)],
                    rhs=w2_words[c][:, D * n : D * (n + 1)].bitcast(FP8X4),
                    rhs_scale=w2_scales[c][:, D * n : D * (n + 1)],
                    start=(i == 0),
                    stop=(i == EG - 1),
                )

        load_logits(0)
        load_h(0, 0)
        load_logits(1)
        load_h(0, 1)
        load_h(1, 0)
        load_w2(0, 0, 2)
        load_h(1, 1)
        for c in range(1, PAIRS - 1):
            load_w2(c, 0, 2)
        for i in range(2):
            load_w2(PAIRS - 1, i, i + 1)
        b2_by_i = b2.rearrange("(g i) d -> i g d", i=EG)
        for i in range(EG):
            nc.sync.dma_start(
                out=bias[S * i : S * (i + 1), :, :],
                in_=b2_by_i[i : i + 1].to_broadcast([S, GROUPS, D]),
            )

        make_identity(nc, ident_f32[:])
        warm_in = keep.tile([P, 1], F32)
        warm_out = keep.tile([P, 1], F32)
        nc.vector.memset(warm_in[:], 0.0)
        nc.scalar.activation(out=warm_out[:], in_=warm_in[:], func=ACT.Exp)
        for b in range(B):
            nc.vector.memset(h_masked[b][:].bitcast(I32).rearrange("p (e x) -> p e x", x=P)[:, :, 0:ZEROS], 0)

        softmax_max(0)
        softmax_max(1)
        softmax_exp(0)
        softmax_exp(1)
        softmax_normalise(0)
        softmax_normalise(1)
        transpose_h(0, 0)
        transpose_h(0, 1)
        transpose_h(1, 0)
        regroup_pair(0)
        transpose_h(1, 1)
        for b in range(B):
            transpose_cw(b)
        quantise_h(0)
        regroup_pair(1)
        mask_h(0)
        quantise_w2(0, 0, 2)
        regroup_pair(2)
        quantise_h(1)
        quantise_w2(1, 0, 2)
        mask_h(1)
        regroup_pair(3)
        for c in range(2):
            for b in range(B):
                expert_passes(c, b)

        for c in range(2, PAIRS - 2):
            quantise_w2(c, 0, 2)
            regroup_pair(c + 2)
            for b in range(B):
                expert_passes(c, b)
        quantise_w2(PAIRS - 2, 0, 2)
        for i in range(2):
            quantise_w2(PAIRS - 1, i, i + 1)
        for b in range(B):
            for c in (PAIRS - 2, PAIRS - 1):
                expert_passes(c, b)

        quantise_cw()

        for b in range(B):
            nc.vector.tensor_tensor(
                out=eo_grp[b][:],
                in0=eo_ps[b][:].rearrange("p g d -> p d g"),
                in1=bias[:].rearrange("p g d -> p d g"),
                op=ALU.add,
            )
        for b in range(B):
            nc.vector.quantize_mx(
                out=eo_words[b][:].bitcast(FP8X4), scales=eo_scales[b][:], in_=eo_grp[b][:].rearrange("p d g -> p (d g)")
            )
        for b in range(B):
            out_ps = psum.tile([P, D], F32, name="out_ps%d" % b, tag="transposed", bufs=4)
            nc.tensor.matmul_mx(
                out=out_ps[:],
                lhsT=cw_words[:, L * b : L * (b + 1)].bitcast(FP8X4),
                lhsT_scale=cw_scales[:, L * b : L * (b + 1)],
                rhs=eo_words[b][:].bitcast(FP8X4),
                rhs_scale=eo_scales[b][:],
                start=True,
                stop=True,
            )
            out_sb = keep.tile([P, D], F32, name="out_sb%d" % b)
            if b == 0:
                nc.scalar.copy(out=out_sb[:], in_=out_ps[:])
            else:
                nc.vector.tensor_copy(out=out_sb[:], in_=out_ps[:])
            nc.sync.dma_start(out=out[b], in_=out_sb[:])
